import numpy as np
import ml_dtypes


def mxq(x, axis, fmt="e4m3"):
    dtype, down = {"e4m3": (ml_dtypes.float8_e4m3fn, 7), "e5m2": (ml_dtypes.float8_e5m2, 14)}[fmt]
    v = np.moveaxis(np.asarray(x, np.float32).astype(ml_dtypes.bfloat16).astype(np.float64), axis, -1)
    blocks = v.reshape(v.shape[:-1] + (-1, 32))
    amax = np.abs(blocks).max(-1, keepdims=True)
    byte = np.maximum(np.where(amax > 0, np.frexp(amax)[1] - 1 + 127, 0) - down, 1)
    scale = np.exp2(byte - 127.0)
    codes = (blocks / scale).astype(np.float32).astype(dtype).astype(np.float64)
    return np.moveaxis((codes * scale).reshape(v.shape), -1, axis)


WIDE = False


def mx_kscale(k):
    if not WIDE:
        return np.ones(k)
    levels = np.array([10, -10, 5, -5, 0])
    if k % 512:
        return np.exp2(np.random.permutation(np.resize(levels, k // 32))).repeat(32)
    a = np.empty((k // 512, 16))
    for p in range(k // 512):
        a[p, :8] = np.random.permutation(np.resize(levels, 8))
        for g in range(8):
            far = levels[np.abs(levels - a[p, g]) >= 10]
            a[p, g + 8] = far[np.random.randint(len(far))]
    return np.exp2(a.ravel()).repeat(32)


BF16 = ml_dtypes.bfloat16


def bf(x):
    return np.asarray(x, np.float32).astype(BF16)


def f64(x):
    return np.asarray(x).astype(np.float64)


NK, F, B = 3072, 512, 128
D = 2 * F
EPS = 1e-8


def rotate_half(x):
    d = x.shape[-1] // 2
    return np.concatenate([-x[..., d:], x[..., :d]], axis=-1)


def setup_inputs():
    sf = mx_kscale(F)
    s = np.concatenate([sf, sf])
    c = np.exp2(np.round(0.5 * np.log2(np.mean(1.0 / s**2))))
    return {"K": bf(np.random.standard_normal((NK, D)) * s * c),
            "reference_angles": bf(np.random.random(F) * 2.0 * np.pi),
            "probes": bf(np.random.standard_normal((B, D)) / s),
            "u_weights": bf(np.random.standard_normal((B, F)) * 0.5 / np.sqrt(F) / (sf * c)),
            "k_bias": bf(np.random.standard_normal(B) * 0.5)}


def reference(K, reference_angles, probes, u_weights, k_bias):
    K = f64(K)
    probes = f64(probes)
    pnorm = np.sqrt(np.sum(probes**2, axis=-1, keepdims=True))
    p = probes / (pnorm + EPS)
    theta_full = np.concatenate([f64(reference_angles), f64(reference_angles)], axis=-1)
    rotated = p * np.cos(theta_full) + rotate_half(p) * np.sin(theta_full)
    dot_term = mxq(K, 1, "e4m3") @ mxq(rotated, 1, "e4m3").T
    K_mag = np.sqrt(K[..., :F] ** 2 + K[..., F:] ** 2 + EPS)
    logits = dot_term + (mxq(K_mag, 1, "e4m3") @ mxq(f64(u_weights), 1, "e4m3").T) + f64(k_bias)
    return logits

@@ -1,0 +1,354 @@
+import math
+from contextlib import ExitStack
+
+import concourse.mybir as mybir
+from concourse.masks import make_identity
+
+F32 = mybir.dt.float32
+BF16 = mybir.dt.bfloat16
+U32 = mybir.dt.uint32
+U8 = mybir.dt.uint8
+FP8X4 = mybir.dt.float8_e4m3fn_x4
+ACT = mybir.ActivationFunctionType
+ALU = mybir.AluOpType
+
+P = 128
+PACK = 4
+ROWS = 3072
+FREQS = 512
+PARTS = 2
+FEATURES = PARTS * FREQS
+ROW_TILES = ROWS // P
+PAIR = 2
+PAIRS = ROW_TILES // PAIR
+EPS = 1e-8
+QUANTISE_LAG = 4
+LAST_STAGE = QUANTISE_LAG + 2
+SCALAR_SQUARES = 3 * FREQS
+
+FLOPS = 2 * ROWS * P * (FEATURES + FREQS)
+
+TWO_PI = 2.0 * math.pi
+TWO_PI_HIGH = 6.28125
+TWO_PI_LOW = TWO_PI - TWO_PI_HIGH
+ROUND_MAGIC = 1.5 * 2.0**23
+
+
+def quantise(nc, values, codes, scales):
+    nc.vector.quantize_mx(out=codes.bitcast(FP8X4), scales=scales, in_=values)
+
+
+def tile_module2network_kernel(tc, K, reference_angles, probes, u_weights, k_bias, out):
+    nc = tc.nc
+    with ExitStack() as ctx:
+        const = ctx.enter_context(tc.tile_pool(name="const", bufs=1))
+        k_pool = ctx.enter_context(tc.tile_pool(name="k_in", bufs=PAIRS))
+        mx_pool = ctx.enter_context(tc.tile_pool(name="mx", bufs=PAIRS))
+        work = ctx.enter_context(tc.tile_pool(name="work", bufs=3))
+        grouped_pool = ctx.enter_context(tc.tile_pool(name="grouped", bufs=QUANTISE_LAG + 2))
+        k_bank_pool = ctx.enter_context(tc.psum_pool(name="k_bank", bufs=4))
+        start_pool = ctx.enter_context(tc.psum_pool(name="start", bufs=2))
+        acc_pool = ctx.enter_context(tc.psum_pool(name="acc", bufs=2))
+        ctx.enter_context(tc.manual_schedule())
+
+        theta = const.tile([P, PACK], BF16)
+        nc.sync.dma_start(out=theta[:], in_=reference_angles.rearrange("(p t) -> p t", t=PACK))
+        probes_sb = const.tile([P, FEATURES], BF16)
+        nc.sync.dma_start(out=probes_sb[:], in_=probes)
+        u_sb = const.tile([P, FREQS], BF16)
+        nc.sync.dma_start(out=u_sb[:], in_=u_weights)
+        k_rows = K.rearrange("(p j) k -> p j k", j=ROW_TILES)
+        k_in = []
+        for i in range(PAIRS):
+            k_pair = k_pool.tile([P, PAIR, FEATURES], BF16, name="k_pair")
+            k_in.append(k_pair)
+            nc.sync.dma_start(out=k_pair[:], in_=k_rows[:, PAIR * i : PAIR * (i + 1), :])
+        bias_rows = const.tile([P, P], BF16)
+        nc.sync.dma_start(out=bias_rows[:], in_=k_bias.partition_broadcast(P))
+
+        zero_col = const.tile([P, 1], F32)
+        nc.gpsimd.memset(zero_col[:], 0.0)
+        warm_col = const.tile([P, 1], F32)
+        nc.scalar.activation(out=warm_col[:], in_=zero_col[:], func=ACT.Sin)
+        ident = const.tile([P, P], F32)
+        make_identity(nc, ident[:])
+        eps_col = const.tile([P, 1], F32)
+        nc.gpsimd.memset(eps_col[:], EPS)
+
+        k_banks = {}
+        k_grouped = {}
+        k_codes = {}
+        k_scales = {}
+        k_squared = {}
+        mag_squared = {}
+        mag_grouped = {}
+        mag_codes = {}
+        mag_scales = {}
+        accs = {}
+        out_rows = out.rearrange("(p j) b -> p j b", j=ROW_TILES)
+        bias_b = bias_rows[:].unsqueeze(1).to_broadcast([P, PAIR, P])
+
+        def exists(i):
+            return 0 <= i < PAIRS
+
+        def transpose_k(i):
+            if not exists(i):
+                return
+            k_words = k_in[i][:].bitcast(F32)
+            k_banks[i] = {}
+            for j in reversed(range(PAIR)):
+                k_bank = k_bank_pool.tile([P, PACK, P], F32, name="k_bank")
+                for g in range(PARTS):
+                    for h in range(2):
+                        nc.tensor.transpose(
+                            k_bank[:, 2 * g + h, :],
+                            k_words[:, j, 2 * P * g + h : 2 * P * (g + 1) : 2],
+                            ident[:],
+                        )
+                k_banks[i][j] = k_bank
+
+        def copy_k(i):
+            if not exists(i):
+                return
+            k_grouped[i] = grouped_pool.tile(
+                [P, PAIR, PARTS, P * PACK], BF16, align_bytes=64, name="k_grouped"
+            )
+            k_grouped_words = k_grouped[i][:].bitcast(F32).rearrange("p j g (n h) -> p j g n h", h=2)
+            for j in reversed(range(PAIR)):
+                nc.vector.tensor_copy(
+                    out=k_grouped_words[:, j],
+                    in_=k_banks[i][j][:].rearrange("p (g h) n -> p g n h", g=PARTS),
+                )
+            k_squared[i] = work.tile([P, PAIR, PARTS, P * PACK], F32, name="k_squared")
+            nc.vector.tensor_tensor(
+                out=k_squared[i][:, PAIR - 1, 1, :].rearrange("p (n h e) -> p n h e", h=2, e=2),
+                in0=k_banks[i][PAIR - 1][:]
+                .bitcast(BF16)[:, 2:PACK, :]
+                .rearrange("p h (n e) -> p n h e", e=2),
+                in1=k_grouped[i][:, PAIR - 1, 1, :].rearrange("p (n h e) -> p n h e", h=2, e=2),
+                op=ALU.mult,
+            )
+
+        def quantise_k(i):
+            if not exists(i):
+                return
+            k_codes[i] = mx_pool.tile([P, PAIR, PARTS, P], U32, align_bytes=64, name="k_codes")
+            k_scales[i] = mx_pool.tile([P, PAIR, PARTS, P], U8, align_bytes=64, name="k_scales")
+            quantise(
+                nc,
+                k_grouped[i][:].rearrange("p j g w -> p (j g w)"),
+                k_codes[i][:].rearrange("p j g n -> p (j g n)"),
+                k_scales[i][:].rearrange("p j g n -> p (j g n)"),
+            )
+
+        def squares(i):
+            if not exists(i):
+                return
+            nc.scalar.activation(
+                out=k_squared[i][:].rearrange("p j g w -> p (j g w)")[:, 0:SCALAR_SQUARES],
+                in_=k_grouped[i][:].rearrange("p j g w -> p (j g w)")[:, 0:SCALAR_SQUARES],
+                func=ACT.Square,
+            )
+
+        def sums(i):
+            if not exists(i):
+                return
+            mag_squared[i] = work.tile([P, PAIR, P * PACK], F32, name="mag_squared")
+            nc.gpsimd.tensor_tensor(
+                out=mag_squared[i][:],
+                in0=k_squared[i][:, :, 0, :],
+                in1=k_squared[i][:, :, 1, :],
+                op=ALU.add,
+            )
+
+        def roots(i):
+            if not exists(i):
+                return
+            mag_grouped[i] = work.tile([P, PAIR, P * PACK], BF16, align_bytes=64, name="mag_grouped")
+            nc.scalar.activation(
+                out=mag_grouped[i][:], in_=mag_squared[i][:], func=ACT.Sqrt, bias=eps_col[:, 0:1]
+            )
+
+        def quantise_mag(i):
+            if not exists(i):
+                return
+            mag_codes[i] = mx_pool.tile([P, PAIR, P], U32, align_bytes=64, name="mag_codes")
+            mag_scales[i] = mx_pool.tile([P, PAIR, P], U8, align_bytes=64, name="mag_scales")
+            quantise(
+                nc,
+                mag_grouped[i][:].rearrange("p j w -> p (j w)"),
+                mag_codes[i][:].rearrange("p j n -> p (j n)"),
+                mag_scales[i][:].rearrange("p j n -> p (j n)"),
+            )
+
+        def products(i):
+            if not exists(i):
+                return
+            accs[i] = acc_pool.tile([P, PAIR, P], F32, name="acc")
+            for j in range(PAIR):
+                for g in range(PARTS):
+                    nc.tensor.matmul_mx(
+                        out=accs[i][:, j, :],
+                        lhsT=k_codes[i][:, j, g, :].bitcast(FP8X4),
+                        lhsT_scale=k_scales[i][:, j, g, :],
+                        rhs=rot_codes[:, g, :].bitcast(FP8X4),
+                        rhs_scale=rot_scales[:, g, :],
+                        start=(g == 0),
+                        stop=False,
+                    )
+                nc.tensor.matmul_mx(
+                    out=accs[i][:, j, :],
+                    lhsT=mag_codes[i][:, j, :].bitcast(FP8X4),
+                    lhsT_scale=mag_scales[i][:, j, :],
+                    rhs=u_codes[:].bitcast(FP8X4),
+                    rhs_scale=u_scales[:],
+                    start=False,
+                    stop=True,
+                )
+
+        def finish(i):
+            if not exists(i):
+                return
+            logits = work.tile([P, PAIR, P], F32, name="logits")
+            nc.vector.tensor_tensor(out=logits[:], in0=accs[i][:], in1=bias_b, op=ALU.add)
+            nc.sync.dma_start(out=out_rows[:, PAIR * i : PAIR * (i + 1), :], in_=logits[:])
+
+        def step(s):
+            transpose_k(s + 1)
+            copy_k(s)
+            squares(s - 1)
+            sums(s - 2)
+            quantise_k(s - QUANTISE_LAG)
+            roots(s - 3)
+            quantise_mag(s - QUANTISE_LAG)
+            products(s - QUANTISE_LAG - 1)
+            finish(s - LAST_STAGE)
+
+        angle = const.tile([P, 2 * PACK], F32)
+        nc.vector.tensor_scalar(
+            out=angle[:, 0:PACK], in0=theta[:], scalar1=1.0, scalar2=0.0, op0=ALU.mult, op1=ALU.add
+        )
+        nc.vector.tensor_scalar(
+            out=angle[:, PACK : 2 * PACK],
+            in0=theta[:],
+            scalar1=1.0,
+            scalar2=0.5 * math.pi,
+            op0=ALU.mult,
+            op1=ALU.add,
+        )
+        turns = const.tile([P, 2 * PACK], F32)
+        nc.vector.tensor_scalar(
+            out=turns[:],
+            in0=angle[:],
+            scalar1=1.0 / TWO_PI,
+            scalar2=ROUND_MAGIC,
+            op0=ALU.mult,
+            op1=ALU.add,
+        )
+        off_high = const.tile([P, 2 * PACK], F32)
+        nc.vector.tensor_scalar(
+            out=off_high[:],
+            in0=turns[:],
+            scalar1=-ROUND_MAGIC,
+            scalar2=-TWO_PI_HIGH,
+            op0=ALU.add,
+            op1=ALU.mult,
+        )
+        off_low = const.tile([P, 2 * PACK], F32)
+        nc.vector.tensor_scalar(
+            out=off_low[:],
+            in0=turns[:],
+            scalar1=-ROUND_MAGIC,
+            scalar2=-TWO_PI_LOW,
+            op0=ALU.add,
+            op1=ALU.mult,
+        )
+        reduced_high = const.tile([P, 2 * PACK], F32)
+        nc.vector.tensor_tensor(out=reduced_high[:], in0=angle[:], in1=off_high[:], op=ALU.add)
+        reduced = const.tile([P, 2 * PACK], F32)
+        nc.vector.tensor_tensor(out=reduced[:], in0=reduced_high[:], in1=off_low[:], op=ALU.add)
+
+        probes_squared = const.tile([P, FEATURES], BF16)
+        sum_squares = const.tile([P, 1], F32)
+        nc.scalar.activation(
+            out=probes_squared[:], in_=probes_sb[:], func=ACT.Square, accum_out=sum_squares[:]
+        )
+        sin_cos = const.tile([P, 2 * PACK], F32)
+        nc.scalar.activation(out=sin_cos[:], in_=reduced[:], func=ACT.Sin)
+        sin_b = sin_cos[:, 0:PACK].unsqueeze(2).to_broadcast([P, PACK, P])
+        cos_b = sin_cos[:, PACK : 2 * PACK].unsqueeze(2).to_broadcast([P, PACK, P])
+
+        u_words = u_sb[:].bitcast(F32)
+        u_bank = start_pool.tile([P, PACK, P], F32, tag="start", name="u_bank")
+        for h in range(2):
+            nc.tensor.transpose(u_bank[:, h, :], u_words[:, h : 2 * P : 2], ident[:])
+        u_grouped = const.tile([P, P, PACK], BF16, align_bytes=64)
+        nc.vector.tensor_copy(
+            out=u_grouped[:].bitcast(F32), in_=u_bank[:, 0:2, :].rearrange("p h b -> p b h")
+        )
+        u_codes = const.tile([P, P], U32, align_bytes=64)
+        u_scales = const.tile([P, P], U8, align_bytes=64)
+        quantise(nc, u_grouped[:].rearrange("p b t -> p (b t)"), u_codes[:], u_scales[:])
+
+        step(-1)
+        step(0)
+
+        norm = const.tile([P, 1], F32)
+        nc.scalar.activation(out=norm[:], in_=sum_squares[:], func=ACT.Sqrt)
+        norm_eps = const.tile([P, 1], F32)
+        nc.vector.tensor_scalar_add(out=norm_eps[:], in0=norm[:], scalar1=EPS)
+        inv_norm = const.tile([P, 1], F32)
+        nc.vector.reciprocal(out=inv_norm[:], in_=norm_eps[:])
+        p_unit = const.tile([P, FEATURES], F32)
+        nc.vector.tensor_scalar_mul(out=p_unit[:], in0=probes_sb[:], scalar1=inv_norm[:, 0:1])
+        p_cols = p_unit[:].rearrange("b (g q t) -> b g q t", g=PARTS, t=PACK)
+        p_banks = []
+        for g in range(PARTS):
+            p_bank = start_pool.tile([P, PACK, P], F32, tag="start", name="p_bank")
+            for t in range(PACK):
+                nc.tensor.transpose(p_bank[:, t, :], p_cols[:, g, :, t], ident[:])
+            p_banks.append(p_bank)
+
+        step(1)
+
+        re_cos = const.tile([P, PACK, P], F32)
+        nc.vector.tensor_tensor(out=re_cos[:], in0=p_banks[0][:], in1=cos_b, op=ALU.mult)
+        im_sin = const.tile([P, PACK, P], F32)
+        nc.vector.tensor_tensor(out=im_sin[:], in0=p_banks[1][:], in1=sin_b, op=ALU.mult)
+
+        step(2)
+
+        im_cos = const.tile([P, PACK, P], F32)
+        nc.vector.tensor_tensor(out=im_cos[:], in0=p_banks[1][:], in1=cos_b, op=ALU.mult)
+        re_sin = const.tile([P, PACK, P], F32)
+        nc.vector.tensor_tensor(out=re_sin[:], in0=p_banks[0][:], in1=sin_b, op=ALU.mult)
+
+        step(3)
+
+        rot_grouped = const.tile([P, PARTS, P, PACK], BF16, align_bytes=64)
+        nc.vector.tensor_tensor(
+            out=rot_grouped[:, 0],
+            in0=re_cos[:].rearrange("p t b -> p b t"),
+            in1=im_sin[:].rearrange("p t b -> p b t"),
+            op=ALU.subtract,
+        )
+        nc.vector.tensor_tensor(
+            out=rot_grouped[:, 1],
+            in0=im_cos[:].rearrange("p t b -> p b t"),
+            in1=re_sin[:].rearrange("p t b -> p b t"),
+            op=ALU.add,
+        )
+
+        step(4)
+
+        rot_codes = const.tile([P, PARTS, P], U32, align_bytes=64)
+        rot_scales = const.tile([P, PARTS, P], U8, align_bytes=64)
+        quantise(
+            nc,
+            rot_grouped[:].rearrange("p g b t -> p (g b t)"),
+            rot_codes[:].rearrange("p g b -> p (g b)"),
+            rot_scales[:].rearrange("p g b -> p (g b)"),
+        )
+
+        for s in range(QUANTISE_LAG + 1, PAIRS + LAST_STAGE):
+            step(s)

@@ -24,7 +24,6 @@ PAIRS = ROW_TILES // PAIR
 EPS = 1e-8
 QUANTISE_LAG = 4
 LAST_STAGE = QUANTISE_LAG + 2
-SCALAR_SQUARES = 3 * FREQS
 
 FLOPS = 2 * ROWS * P * (FEATURES + FREQS)
 
@@ -119,15 +118,6 @@ def tile_module2network_kernel(tc, K, reference_angles, probes, u_weights, k_bia
                     out=k_grouped_words[:, j],
                     in_=k_banks[i][j][:].rearrange("p (g h) n -> p g n h", g=PARTS),
                 )
-            k_squared[i] = work.tile([P, PAIR, PARTS, P * PACK], F32, name="k_squared")
-            nc.vector.tensor_tensor(
-                out=k_squared[i][:, PAIR - 1, 1, :].rearrange("p (n h e) -> p n h e", h=2, e=2),
-                in0=k_banks[i][PAIR - 1][:]
-                .bitcast(BF16)[:, 2:PACK, :]
-                .rearrange("p h (n e) -> p n h e", e=2),
-                in1=k_grouped[i][:, PAIR - 1, 1, :].rearrange("p (n h e) -> p n h e", h=2, e=2),
-                op=ALU.mult,
-            )
 
         def quantise_k(i):
             if not exists(i):
@@ -144,9 +134,10 @@ def tile_module2network_kernel(tc, K, reference_angles, probes, u_weights, k_bia
         def squares(i):
             if not exists(i):
                 return
+            k_squared[i] = work.tile([P, PAIR, PARTS, P * PACK], F32, name="k_squared")
             nc.scalar.activation(
-                out=k_squared[i][:].rearrange("p j g w -> p (j g w)")[:, 0:SCALAR_SQUARES],
-                in_=k_grouped[i][:].rearrange("p j g w -> p (j g w)")[:, 0:SCALAR_SQUARES],
+                out=k_squared[i][:].rearrange("p j g w -> p (j g w)"),
+                in_=k_grouped[i][:].rearrange("p j g w -> p (j g w)"),
                 func=ACT.Square,
             )
 
@@ -154,7 +145,7 @@ def tile_module2network_kernel(tc, K, reference_angles, probes, u_weights, k_bia
             if not exists(i):
                 return
             mag_squared[i] = work.tile([P, PAIR, P * PACK], F32, name="mag_squared")
-            nc.gpsimd.tensor_tensor(
+            nc.vector.tensor_tensor(
                 out=mag_squared[i][:],
                 in0=k_squared[i][:, :, 0, :],
                 in1=k_squared[i][:, :, 1, :],

@@ -145,12 +145,16 @@ def tile_module2network_kernel(tc, K, reference_angles, probes, u_weights, k_bia
             if not exists(i):
                 return
             mag_squared[i] = work.tile([P, PAIR, P * PACK], F32, name="mag_squared")
-            nc.vector.tensor_tensor(
-                out=mag_squared[i][:],
-                in0=k_squared[i][:, :, 0, :],
-                in1=k_squared[i][:, :, 1, :],
-                op=ALU.add,
-            )
+            if exists(i + 1 - QUANTISE_LAG):
+                gate = work.tile([P, 1], U32, name="gate")
+                nc.gpsimd.tensor_copy(out=gate[:], in_=mag_codes[i + 1 - QUANTISE_LAG][:, 0, 0:1])
+            for engine, j in ((nc.gpsimd, 0), (nc.vector, 1)):
+                engine.tensor_tensor(
+                    out=mag_squared[i][:, j, :],
+                    in0=k_squared[i][:, j, 0, :],
+                    in1=k_squared[i][:, j, 1, :],
+                    op=ALU.add,
+                )
 
         def roots(i):
             if not exists(i):
@@ -207,13 +211,13 @@ def tile_module2network_kernel(tc, K, reference_angles, probes, u_weights, k_bia
         def step(s):
             transpose_k(s + 1)
             copy_k(s)
+            finish(s - LAST_STAGE)
             squares(s - 1)
             sums(s - 2)
             quantise_k(s - QUANTISE_LAG)
             roots(s - 3)
             quantise_mag(s - QUANTISE_LAG)
             products(s - QUANTISE_LAG - 1)
-            finish(s - LAST_STAGE)
 
         angle = const.tile([P, 2 * PACK], F32)
         nc.vector.tensor_scalar(

@@ -22,8 +22,17 @@ ROW_TILES = ROWS // P
 PAIR = 2
 PAIRS = ROW_TILES // PAIR
 EPS = 1e-8
-QUANTISE_LAG = 4
-LAST_STAGE = QUANTISE_LAG + 2
+VECTOR_SQUARES = 128
+SCALAR_SQUARES = PAIR * FEATURES - VECTOR_SQUARES
+TRANSPOSE_LEAD = 2
+COPY_LEAD = 1
+ADD_LAG = 1
+TENSOR_ADD_LAG = 2
+ROOT_LAG = 3
+QUANTISE_K_LAG = 3
+QUANTISE_MAG_LAG = 4
+PRODUCT_LAG = 5
+FINISH_LAG = 6
 
 FLOPS = 2 * ROWS * P * (FEATURES + FREQS)
 
@@ -31,22 +40,90 @@ TWO_PI = 2.0 * math.pi
 TWO_PI_HIGH = 6.28125
 TWO_PI_LOW = TWO_PI - TWO_PI_HIGH
 ROUND_MAGIC = 1.5 * 2.0**23
+SINE = [(-1.0) ** k / math.factorial(2 * k + 1) for k in range(11)]
+
+
+def in_own_layout(i):
+    return i == 0 or i % 4 == 1
+
+
+def row_tile_groups(i):
+    return [slice(0, PAIR)] if i < PAIRS - 1 else [slice(j, j + 1) for j in range(PAIR)]
+
+
+def exists(i):
+    return 0 <= i < PAIRS
+
+
+def due(s, lag):
+    if s - lag == 1:
+        return [0, 1]
+    return [s - lag] if exists(s - lag) and s > lag else []
 
 
 def quantise(nc, values, codes, scales):
     nc.vector.quantize_mx(out=codes.bitcast(FP8X4), scales=scales, in_=values)
 
 
+def sine(nc, pool, theta):
+    width = 2 * PACK
+    angle = pool.tile([P, width], F32, name="angle")
+    for half, offset in ((0, 0.0), (1, 0.5 * math.pi)):
+        nc.vector.tensor_scalar(
+            out=angle[:, PACK * half : PACK * (half + 1)],
+            in0=theta[:],
+            scalar1=1.0,
+            scalar2=offset,
+            op0=ALU.mult,
+            op1=ALU.add,
+        )
+    shifted = pool.tile([P, width], F32, name="shifted")
+    nc.vector.tensor_scalar(
+        out=shifted[:], in0=angle[:], scalar1=1.0 / TWO_PI, scalar2=ROUND_MAGIC, op0=ALU.mult, op1=ALU.add
+    )
+    turns = pool.tile([P, width], F32, name="turns")
+    nc.vector.tensor_scalar(
+        out=turns[:], in0=shifted[:], scalar1=-ROUND_MAGIC, scalar2=1.0, op0=ALU.add, op1=ALU.mult
+    )
+    x = angle
+    for part in (TWO_PI_HIGH, TWO_PI_LOW):
+        reduced = pool.tile([P, width], F32, name="reduced")
+        nc.vector.scalar_tensor_tensor(
+            out=reduced[:], in0=turns[:], scalar=-part, in1=x[:], op0=ALU.mult, op1=ALU.add
+        )
+        x = reduced
+    x_squared = pool.tile([P, width], F32, name="x_squared")
+    nc.vector.tensor_tensor(out=x_squared[:], in0=x[:], in1=x[:], op=ALU.mult)
+    partial = x_squared
+    factor = SINE[-1]
+    for k in reversed(range(len(SINE) - 1)):
+        series = pool.tile([P, width], F32, name="series")
+        nc.gpsimd.tensor_scalar(
+            out=series[:], in0=partial[:], scalar1=factor, scalar2=SINE[k], op0=ALU.mult, op1=ALU.add
+        )
+        product = pool.tile([P, width], F32, name="product")
+        nc.gpsimd.tensor_tensor(
+            out=product[:], in0=series[:], in1=x_squared[:] if k > 0 else x[:], op=ALU.mult
+        )
+        partial = product
+        factor = 1.0
+    return partial
+
+
 def tile_module2network_kernel(tc, K, reference_angles, probes, u_weights, k_bias, out):
     nc = tc.nc
     with ExitStack() as ctx:
         const = ctx.enter_context(tc.tile_pool(name="const", bufs=1))
+        small = ctx.enter_context(tc.tile_pool(name="small", bufs=2))
         k_pool = ctx.enter_context(tc.tile_pool(name="k_in", bufs=PAIRS))
         mx_pool = ctx.enter_context(tc.tile_pool(name="mx", bufs=PAIRS))
-        work = ctx.enter_context(tc.tile_pool(name="work", bufs=3))
-        grouped_pool = ctx.enter_context(tc.tile_pool(name="grouped", bufs=QUANTISE_LAG + 2))
+        work = ctx.enter_context(tc.tile_pool(name="work", bufs=4))
+        own_pool = ctx.enter_context(tc.tile_pool(name="own", bufs=2))
+        grouped_pool = ctx.enter_context(
+            tc.tile_pool(name="grouped", bufs=COPY_LEAD + QUANTISE_K_LAG + 2)
+        )
         k_bank_pool = ctx.enter_context(tc.psum_pool(name="k_bank", bufs=4))
-        start_pool = ctx.enter_context(tc.psum_pool(name="start", bufs=2))
+        sum_pool = ctx.enter_context(tc.psum_pool(name="sum", bufs=2))
         acc_pool = ctx.enter_context(tc.psum_pool(name="acc", bufs=2))
         ctx.enter_context(tc.manual_schedule())
 
@@ -55,20 +132,25 @@ def tile_module2network_kernel(tc, K, reference_angles, probes, u_weights, k_bia
         probes_sb = const.tile([P, FEATURES], BF16)
         nc.sync.dma_start(out=probes_sb[:], in_=probes)
         u_sb = const.tile([P, FREQS], BF16)
-        nc.sync.dma_start(out=u_sb[:], in_=u_weights)
         k_rows = K.rearrange("(p j) k -> p j k", j=ROW_TILES)
         k_in = []
         for i in range(PAIRS):
             k_pair = k_pool.tile([P, PAIR, FEATURES], BF16, name="k_pair")
             k_in.append(k_pair)
-            nc.sync.dma_start(out=k_pair[:], in_=k_rows[:, PAIR * i : PAIR * (i + 1), :])
+            if i == 0:
+                for j in range(PAIR):
+                    nc.sync.dma_start(out=k_pair[:, j, :], in_=k_rows[:, j, :])
+            else:
+                nc.sync.dma_start(out=k_pair[:], in_=k_rows[:, PAIR * i : PAIR * (i + 1), :])
+            if i == 1:
+                nc.sync.dma_start(out=u_sb[:], in_=u_weights)
         bias_rows = const.tile([P, P], BF16)
         nc.sync.dma_start(out=bias_rows[:], in_=k_bias.partition_broadcast(P))
 
         zero_col = const.tile([P, 1], F32)
         nc.gpsimd.memset(zero_col[:], 0.0)
         warm_col = const.tile([P, 1], F32)
-        nc.scalar.activation(out=warm_col[:], in_=zero_col[:], func=ACT.Sin)
+        nc.scalar.activation(out=warm_col[:], in_=zero_col[:], func=ACT.Sqrt)
         ident = const.tile([P, P], F32)
         make_identity(nc, ident[:])
         eps_col = const.tile([P, 1], F32)
@@ -79,16 +161,13 @@ def tile_module2network_kernel(tc, K, reference_angles, probes, u_weights, k_bia
         k_codes = {}
         k_scales = {}
         k_squared = {}
+        sum_banks = {}
         mag_squared = {}
         mag_grouped = {}
         mag_codes = {}
         mag_scales = {}
         accs = {}
         out_rows = out.rearrange("(p j) b -> p j b", j=ROW_TILES)
-        bias_b = bias_rows[:].unsqueeze(1).to_broadcast([P, PAIR, P])
-
-        def exists(i):
-            return 0 <= i < PAIRS
 
         def transpose_k(i):
             if not exists(i):
@@ -118,6 +197,105 @@ def tile_module2network_kernel(tc, K, reference_angles, probes, u_weights, k_bia
                     out=k_grouped_words[:, j],
                     in_=k_banks[i][j][:].rearrange("p (g h) n -> p g n h", g=PARTS),
                 )
+            if in_own_layout(i):
+                return
+            k_squared[i] = work.tile([P, PAIR, PARTS, P * PACK], F32, name="k_squared")
+            first_row = P - VECTOR_SQUARES // PACK
+            last = slice(PACK * first_row, PACK * P)
+            nc.vector.tensor_tensor(
+                out=k_squared[i][:, PAIR - 1, 1, last].rearrange("p (n h e) -> p n h e", h=2, e=2),
+                in0=k_banks[i][PAIR - 1][:]
+                .bitcast(BF16)[:, 2:PACK, 2 * first_row :]
+                .rearrange("p h (n e) -> p n h e", e=2),
+                in1=k_grouped[i][:, PAIR - 1, 1, last].rearrange("p (n h e) -> p n h e", h=2, e=2),
+                op=ALU.mult,
+            )
+
+        def squares(i):
+            if not exists(i):
+                return
+            if in_own_layout(i):
+                k_squared[i] = own_pool.tile([P, PAIR, PARTS, PACK, P], F32, name="k_own_squared")
+                nc.scalar.activation(
+                    out=k_squared[i][:].rearrange("r j g t q -> r (j g) t q"),
+                    in_=k_in[i][:].rearrange("r j (g q t) -> r (j g) t q", g=PARTS, t=PACK),
+                    func=ACT.Square,
+                )
+                return
+            out_flat = k_squared[i][:].rearrange("p j g w -> p (j g w)")
+            in_flat = k_grouped[i][:].rearrange("p j g w -> p (j g w)")
+            for js in row_tile_groups(i):
+                cols = slice(js.start * FEATURES, min(js.stop * FEATURES, SCALAR_SQUARES))
+                nc.scalar.activation(out=out_flat[:, cols], in_=in_flat[:, cols], func=ACT.Square)
+
+        def add_on_tensor(i):
+            if not exists(i) or not in_own_layout(i):
+                return
+            sum_banks[i] = {}
+            for j in range(PAIR):
+                sum_bank = sum_pool.tile([P, PACK, P], F32, tag="sum", name="sum_bank")
+                for t in range(PACK):
+                    for g in range(PARTS):
+                        nc.tensor.matmul(
+                            sum_bank[:, t, :],
+                            lhsT=k_squared[i][:, j, g, t, :],
+                            rhs=ident[:],
+                            is_transpose=True,
+                            start=(g == 0),
+                            stop=(g == PARTS - 1),
+                        )
+                sum_banks[i][j] = sum_bank
+
+        def add(i):
+            if not exists(i) or in_own_layout(i):
+                return
+            mag_squared[i] = work.tile([P, PAIR, P * PACK], F32, name="mag_squared")
+            quantised = i + ADD_LAG - 1 - QUANTISE_K_LAG
+            if exists(quantised):
+                gate = small.tile([P, 1], U32, name="gate")
+                nc.gpsimd.tensor_copy(out=gate[:], in_=k_codes[quantised][:, 0, 0, 0:1])
+            for j in range(PAIR):
+                engine = nc.gpsimd if j == 0 and i < PAIRS - 1 else nc.vector
+                engine.tensor_tensor(
+                    out=mag_squared[i][:, j, :],
+                    in0=k_squared[i][:, j, 0, :],
+                    in1=k_squared[i][:, j, 1, :],
+                    op=ALU.add,
+                )
+
+        def roots(i):
+            if not exists(i):
+                return
+            mag_grouped[i] = work.tile([P, PAIR, P * PACK], BF16, align_bytes=64, name="mag_grouped")
+            if in_own_layout(i):
+                for j in range(PAIR):
+                    nc.scalar.activation(
+                        out=mag_grouped[i][:, j, :].rearrange("p (n t) -> p n t", t=PACK),
+                        in_=sum_banks[i][j][:].rearrange("p t n -> p n t"),
+                        func=ACT.Sqrt,
+                        bias=eps_col[:, 0:1],
+                    )
+                return
+            for js in row_tile_groups(i):
+                nc.scalar.activation(
+                    out=mag_grouped[i][:, js, :],
+                    in_=mag_squared[i][:, js, :],
+                    func=ACT.Sqrt,
+                    bias=eps_col[:, 0:1],
+                )
+
+        def quantise_mag(i):
+            if not exists(i):
+                return
+            mag_codes[i] = mx_pool.tile([P, PAIR, P], U32, align_bytes=64, name="mag_codes")
+            mag_scales[i] = mx_pool.tile([P, PAIR, P], U8, align_bytes=64, name="mag_scales")
+            for js in row_tile_groups(i):
+                quantise(
+                    nc,
+                    mag_grouped[i][:, js, :].rearrange("p j w -> p (j w)"),
+                    mag_codes[i][:, js, :].rearrange("p j n -> p (j n)"),
+                    mag_scales[i][:, js, :].rearrange("p j n -> p (j n)"),
+                )
 
         def quantise_k(i):
             if not exists(i):
@@ -131,210 +309,145 @@ def tile_module2network_kernel(tc, K, reference_angles, probes, u_weights, k_bia
                 k_scales[i][:].rearrange("p j g n -> p (j g n)"),
             )
 
-        def squares(i):
-            if not exists(i):
-                return
-            k_squared[i] = work.tile([P, PAIR, PARTS, P * PACK], F32, name="k_squared")
-            nc.scalar.activation(
-                out=k_squared[i][:].rearrange("p j g w -> p (j g w)"),
-                in_=k_grouped[i][:].rearrange("p j g w -> p (j g w)"),
-                func=ACT.Square,
-            )
-
-        def sums(i):
-            if not exists(i):
-                return
-            mag_squared[i] = work.tile([P, PAIR, P * PACK], F32, name="mag_squared")
-            if exists(i + 1 - QUANTISE_LAG):
-                gate = work.tile([P, 1], U32, name="gate")
-                nc.gpsimd.tensor_copy(out=gate[:], in_=mag_codes[i + 1 - QUANTISE_LAG][:, 0, 0:1])
-            for engine, j in ((nc.gpsimd, 0), (nc.vector, 1)):
-                engine.tensor_tensor(
-                    out=mag_squared[i][:, j, :],
-                    in0=k_squared[i][:, j, 0, :],
-                    in1=k_squared[i][:, j, 1, :],
-                    op=ALU.add,
-                )
-
-        def roots(i):
-            if not exists(i):
-                return
-            mag_grouped[i] = work.tile([P, PAIR, P * PACK], BF16, align_bytes=64, name="mag_grouped")
-            nc.scalar.activation(
-                out=mag_grouped[i][:], in_=mag_squared[i][:], func=ACT.Sqrt, bias=eps_col[:, 0:1]
-            )
-
-        def quantise_mag(i):
-            if not exists(i):
-                return
-            mag_codes[i] = mx_pool.tile([P, PAIR, P], U32, align_bytes=64, name="mag_codes")
-            mag_scales[i] = mx_pool.tile([P, PAIR, P], U8, align_bytes=64, name="mag_scales")
-            quantise(
-                nc,
-                mag_grouped[i][:].rearrange("p j w -> p (j w)"),
-                mag_codes[i][:].rearrange("p j n -> p (j n)"),
-                mag_scales[i][:].rearrange("p j n -> p (j n)"),
-            )
-
         def products(i):
             if not exists(i):
                 return
-            accs[i] = acc_pool.tile([P, PAIR, P], F32, name="acc")
-            for j in range(PAIR):
-                for g in range(PARTS):
+            accs[i] = []
+            for js in row_tile_groups(i):
+                acc = acc_pool.tile([P, js.stop - js.start, P], F32, tag="acc", name="acc")
+                accs[i].append(acc)
+                for j in range(js.start, js.stop):
+                    for g in range(PARTS):
+                        nc.tensor.matmul_mx(
+                            out=acc[:, j - js.start, :],
+                            lhsT=k_codes[i][:, j, g, :].bitcast(FP8X4),
+                            lhsT_scale=k_scales[i][:, j, g, :],
+                            rhs=rot_codes[:, g, :].bitcast(FP8X4),
+                            rhs_scale=rot_scales[:, g, :],
+                            start=(g == 0),
+                            stop=False,
+                        )
                     nc.tensor.matmul_mx(
-                        out=accs[i][:, j, :],
-                        lhsT=k_codes[i][:, j, g, :].bitcast(FP8X4),
-                        lhsT_scale=k_scales[i][:, j, g, :],
-                        rhs=rot_codes[:, g, :].bitcast(FP8X4),
-                        rhs_scale=rot_scales[:, g, :],
-                        start=(g == 0),
-                        stop=False,
+                        out=acc[:, j - js.start, :],
+                        lhsT=mag_codes[i][:, j, :].bitcast(FP8X4),
+                        lhsT_scale=mag_scales[i][:, j, :],
+                        rhs=u_codes[:].bitcast(FP8X4),
+                        rhs_scale=u_scales[:],
+                        start=False,
+                        stop=True,
                     )
-                nc.tensor.matmul_mx(
-                    out=accs[i][:, j, :],
-                    lhsT=mag_codes[i][:, j, :].bitcast(FP8X4),
-                    lhsT_scale=mag_scales[i][:, j, :],
-                    rhs=u_codes[:].bitcast(FP8X4),
-                    rhs_scale=u_scales[:],
-                    start=False,
-                    stop=True,
-                )
 
         def finish(i):
             if not exists(i):
                 return
-            logits = work.tile([P, PAIR, P], F32, name="logits")
-            nc.vector.tensor_tensor(out=logits[:], in0=accs[i][:], in1=bias_b, op=ALU.add)
-            nc.sync.dma_start(out=out_rows[:, PAIR * i : PAIR * (i + 1), :], in_=logits[:])
+            for js, acc in zip(row_tile_groups(i), accs[i]):
+                n = js.stop - js.start
+                logits = work.tile([P, n, P], F32, name="logits")
+                bias_b = bias_rows[:].unsqueeze(1).to_broadcast([P, n, P])
+                nc.vector.tensor_tensor(out=logits[:], in0=acc[:], in1=bias_b, op=ALU.add)
+                nc.sync.dma_start(
+                    out=out_rows[:, PAIR * i + js.start : PAIR * i + js.stop, :], in_=logits[:]
+                )
 
-        def step(s):
-            transpose_k(s + 1)
-            copy_k(s)
-            finish(s - LAST_STAGE)
-            squares(s - 1)
-            sums(s - 2)
-            quantise_k(s - QUANTISE_LAG)
-            roots(s - 3)
-            quantise_mag(s - QUANTISE_LAG)
-            products(s - QUANTISE_LAG - 1)
+        def step_on_psum(s):
+            copy_k(s + COPY_LEAD)
+            transpose_k(s + TRANSPOSE_LEAD)
+            for i in due(s, FINISH_LAG):
+                finish(i)
+            squares(s)
 
-        angle = const.tile([P, 2 * PACK], F32)
-        nc.vector.tensor_scalar(
-            out=angle[:, 0:PACK], in0=theta[:], scalar1=1.0, scalar2=0.0, op0=ALU.mult, op1=ALU.add
-        )
-        nc.vector.tensor_scalar(
-            out=angle[:, PACK : 2 * PACK],
-            in0=theta[:],
-            scalar1=1.0,
-            scalar2=0.5 * math.pi,
-            op0=ALU.mult,
-            op1=ALU.add,
-        )
-        turns = const.tile([P, 2 * PACK], F32)
-        nc.vector.tensor_scalar(
-            out=turns[:],
-            in0=angle[:],
-            scalar1=1.0 / TWO_PI,
-            scalar2=ROUND_MAGIC,
-            op0=ALU.mult,
-            op1=ALU.add,
-        )
-        off_high = const.tile([P, 2 * PACK], F32)
-        nc.vector.tensor_scalar(
-            out=off_high[:],
-            in0=turns[:],
-            scalar1=-ROUND_MAGIC,
-            scalar2=-TWO_PI_HIGH,
-            op0=ALU.add,
-            op1=ALU.mult,
-        )
-        off_low = const.tile([P, 2 * PACK], F32)
-        nc.vector.tensor_scalar(
-            out=off_low[:],
-            in0=turns[:],
-            scalar1=-ROUND_MAGIC,
-            scalar2=-TWO_PI_LOW,
-            op0=ALU.add,
-            op1=ALU.mult,
-        )
-        reduced_high = const.tile([P, 2 * PACK], F32)
-        nc.vector.tensor_tensor(out=reduced_high[:], in0=angle[:], in1=off_high[:], op=ALU.add)
-        reduced = const.tile([P, 2 * PACK], F32)
-        nc.vector.tensor_tensor(out=reduced[:], in0=reduced_high[:], in1=off_low[:], op=ALU.add)
+        def step_on_sbuf(s):
+            add_on_tensor(s - TENSOR_ADD_LAG)
+            add(s - ADD_LAG)
+            roots(s - ROOT_LAG)
+            quantise_mag(s - QUANTISE_MAG_LAG)
+            quantise_k(s - QUANTISE_K_LAG)
+            for i in due(s, PRODUCT_LAG):
+                products(i)
+
+        sin_cos = sine(nc, small, theta)
 
         probes_squared = const.tile([P, FEATURES], BF16)
         sum_squares = const.tile([P, 1], F32)
         nc.scalar.activation(
             out=probes_squared[:], in_=probes_sb[:], func=ACT.Square, accum_out=sum_squares[:]
         )
-        sin_cos = const.tile([P, 2 * PACK], F32)
-        nc.scalar.activation(out=sin_cos[:], in_=reduced[:], func=ACT.Sin)
-        sin_b = sin_cos[:, 0:PACK].unsqueeze(2).to_broadcast([P, PACK, P])
-        cos_b = sin_cos[:, PACK : 2 * PACK].unsqueeze(2).to_broadcast([P, PACK, P])
-
-        u_words = u_sb[:].bitcast(F32)
-        u_bank = start_pool.tile([P, PACK, P], F32, tag="start", name="u_bank")
-        for h in range(2):
-            nc.tensor.transpose(u_bank[:, h, :], u_words[:, h : 2 * P : 2], ident[:])
-        u_grouped = const.tile([P, P, PACK], BF16, align_bytes=64)
-        nc.vector.tensor_copy(
-            out=u_grouped[:].bitcast(F32), in_=u_bank[:, 0:2, :].rearrange("p h b -> p b h")
-        )
-        u_codes = const.tile([P, P], U32, align_bytes=64)
-        u_scales = const.tile([P, P], U8, align_bytes=64)
-        quantise(nc, u_grouped[:].rearrange("p b t -> p (b t)"), u_codes[:], u_scales[:])
-
-        step(-1)
-        step(0)
-
         norm = const.tile([P, 1], F32)
         nc.scalar.activation(out=norm[:], in_=sum_squares[:], func=ACT.Sqrt)
         norm_eps = const.tile([P, 1], F32)
         nc.vector.tensor_scalar_add(out=norm_eps[:], in0=norm[:], scalar1=EPS)
         inv_norm = const.tile([P, 1], F32)
         nc.vector.reciprocal(out=inv_norm[:], in_=norm_eps[:])
-        p_unit = const.tile([P, FEATURES], F32)
-        nc.vector.tensor_scalar_mul(out=p_unit[:], in0=probes_sb[:], scalar1=inv_norm[:, 0:1])
-        p_cols = p_unit[:].rearrange("b (g q t) -> b g q t", g=PARTS, t=PACK)
+        p_unit = const.tile([P, PARTS, PACK, P], F32)
+        nc.vector.tensor_scalar_mul(
+            out=p_unit[:],
+            in0=probes_sb[:].rearrange("b (g q t) -> b g t q", g=PARTS, t=PACK),
+            scalar1=inv_norm[:, 0:1],
+        )
+
+        transpose_k(0)
+        transpose_k(1)
         p_banks = []
         for g in range(PARTS):
-            p_bank = start_pool.tile([P, PACK, P], F32, tag="start", name="p_bank")
+            p_bank = acc_pool.tile([P, PACK, P], F32, tag="acc", name="p_bank")
             for t in range(PACK):
-                nc.tensor.transpose(p_bank[:, t, :], p_cols[:, g, :, t], ident[:])
+                nc.tensor.transpose(p_bank[:, t, :], p_unit[:, g, t, :], ident[:])
             p_banks.append(p_bank)
 
-        step(1)
+        copy_k(0)
+        step_on_psum(0)
+        step_on_sbuf(0)
+        step_on_psum(1)
 
+        u_words = u_sb[:].bitcast(F32)
+        u_bank = sum_pool.tile([P, PACK, P], F32, tag="sum", name="u_bank")
+        for h in range(2):
+            nc.tensor.transpose(u_bank[:, h, :], u_words[:, h : 2 * P : 2], ident[:])
+        u_grouped = const.tile([P, P, PACK], BF16, align_bytes=64)
+        nc.vector.tensor_copy(
+            out=u_grouped[:].bitcast(F32), in_=u_bank[:, 0:2, :].rearrange("p h b -> p b h")
+        )
+
+        step_on_sbuf(1)
+        step_on_psum(2)
+
+        u_codes = const.tile([P, P], U32, align_bytes=64)
+        u_scales = const.tile([P, P], U8, align_bytes=64)
+        quantise(nc, u_grouped[:].rearrange("p b t -> p (b t)"), u_codes[:], u_scales[:])
+
+        step_on_sbuf(2)
+        step_on_psum(3)
+
+        sin_b = sin_cos[:, 0:PACK].unsqueeze(2).to_broadcast([P, PACK, P])
+        cos_b = sin_cos[:, PACK : 2 * PACK].unsqueeze(2).to_broadcast([P, PACK, P])
+        rot_grouped = const.tile([P, PARTS, P, PACK], BF16, align_bytes=64)
         re_cos = const.tile([P, PACK, P], F32)
         nc.vector.tensor_tensor(out=re_cos[:], in0=p_banks[0][:], in1=cos_b, op=ALU.mult)
         im_sin = const.tile([P, PACK, P], F32)
         nc.vector.tensor_tensor(out=im_sin[:], in0=p_banks[1][:], in1=sin_b, op=ALU.mult)
-
-        step(2)
-
-        im_cos = const.tile([P, PACK, P], F32)
-        nc.vector.tensor_tensor(out=im_cos[:], in0=p_banks[1][:], in1=cos_b, op=ALU.mult)
-        re_sin = const.tile([P, PACK, P], F32)
-        nc.vector.tensor_tensor(out=re_sin[:], in0=p_banks[0][:], in1=sin_b, op=ALU.mult)
-
-        step(3)
-
-        rot_grouped = const.tile([P, PARTS, P, PACK], BF16, align_bytes=64)
-        nc.vector.tensor_tensor(
+        nc.gpsimd.tensor_tensor(
             out=rot_grouped[:, 0],
             in0=re_cos[:].rearrange("p t b -> p b t"),
             in1=im_sin[:].rearrange("p t b -> p b t"),
             op=ALU.subtract,
         )
-        nc.vector.tensor_tensor(
+
+        step_on_sbuf(3)
+        step_on_psum(4)
+
+        im_cos = const.tile([P, PACK, P], F32)
+        nc.vector.tensor_tensor(out=im_cos[:], in0=p_banks[1][:], in1=cos_b, op=ALU.mult)
+        re_sin = const.tile([P, PACK, P], F32)
+        nc.vector.tensor_tensor(out=re_sin[:], in0=p_banks[0][:], in1=sin_b, op=ALU.mult)
+        nc.gpsimd.tensor_tensor(
             out=rot_grouped[:, 1],
             in0=im_cos[:].rearrange("p t b -> p b t"),
             in1=re_sin[:].rearrange("p t b -> p b t"),
             op=ALU.add,
         )
 
-        step(4)
+        step_on_sbuf(4)
+        step_on_psum(5)
 
         rot_codes = const.tile([P, PARTS, P], U32, align_bytes=64)
         rot_scales = const.tile([P, PARTS, P], U8, align_bytes=64)
@@ -345,5 +458,8 @@ def tile_module2network_kernel(tc, K, reference_angles, probes, u_weights, k_bia
             rot_scales[:].rearrange("p g b -> p (g b)"),
         )
 
-        for s in range(QUANTISE_LAG + 1, PAIRS + LAST_STAGE):
-            step(s)
+        step_on_sbuf(5)
+
+        for s in range(PRODUCT_LAG + 1, PAIRS + FINISH_LAG):
+            step_on_psum(s)
+            step_on_sbuf(s)

@@ -418,33 +418,26 @@ def tile_module2network_kernel(tc, K, reference_angles, probes, u_weights, k_bia
         step_on_sbuf(2)
         step_on_psum(3)
 
-        sin_b = sin_cos[:, 0:PACK].unsqueeze(2).to_broadcast([P, PACK, P])
-        cos_b = sin_cos[:, PACK : 2 * PACK].unsqueeze(2).to_broadcast([P, PACK, P])
+        sin_b = sin_cos[:, 0:PACK].unsqueeze(1).to_broadcast([P, P, PACK])
+        cos_b = sin_cos[:, PACK : 2 * PACK].unsqueeze(1).to_broadcast([P, P, PACK])
+        p_words = [p_bank[:].rearrange("p t b -> p b t") for p_bank in p_banks]
         rot_grouped = const.tile([P, PARTS, P, PACK], BF16, align_bytes=64)
-        re_cos = const.tile([P, PACK, P], F32)
-        nc.vector.tensor_tensor(out=re_cos[:], in0=p_banks[0][:], in1=cos_b, op=ALU.mult)
-        im_sin = const.tile([P, PACK, P], F32)
-        nc.vector.tensor_tensor(out=im_sin[:], in0=p_banks[1][:], in1=sin_b, op=ALU.mult)
+        re_cos = const.tile([P, P, PACK], F32)
+        nc.vector.tensor_tensor(out=re_cos[:], in0=p_words[0], in1=cos_b, op=ALU.mult)
+        im_sin = const.tile([P, P, PACK], F32)
+        nc.vector.tensor_tensor(out=im_sin[:], in0=p_words[1], in1=sin_b, op=ALU.mult)
         nc.gpsimd.tensor_tensor(
-            out=rot_grouped[:, 0],
-            in0=re_cos[:].rearrange("p t b -> p b t"),
-            in1=im_sin[:].rearrange("p t b -> p b t"),
-            op=ALU.subtract,
+            out=rot_grouped[:, 0], in0=re_cos[:], in1=im_sin[:], op=ALU.subtract
         )
 
         step_on_sbuf(3)
         step_on_psum(4)
 
-        im_cos = const.tile([P, PACK, P], F32)
-        nc.vector.tensor_tensor(out=im_cos[:], in0=p_banks[1][:], in1=cos_b, op=ALU.mult)
-        re_sin = const.tile([P, PACK, P], F32)
-        nc.vector.tensor_tensor(out=re_sin[:], in0=p_banks[0][:], in1=sin_b, op=ALU.mult)
-        nc.gpsimd.tensor_tensor(
-            out=rot_grouped[:, 1],
-            in0=im_cos[:].rearrange("p t b -> p b t"),
-            in1=re_sin[:].rearrange("p t b -> p b t"),
-            op=ALU.add,
-        )
+        im_cos = const.tile([P, P, PACK], F32)
+        nc.vector.tensor_tensor(out=im_cos[:], in0=p_words[1], in1=cos_b, op=ALU.mult)
+        re_sin = const.tile([P, P, PACK], F32)
+        nc.vector.tensor_tensor(out=re_sin[:], in0=p_words[0], in1=sin_b, op=ALU.mult)
+        nc.gpsimd.tensor_tensor(out=rot_grouped[:, 1], in0=im_cos[:], in1=re_sin[:], op=ALU.add)
 
         step_on_sbuf(4)
         step_on_psum(5)

import math
from contextlib import ExitStack

import concourse.mybir as mybir
from concourse.masks import make_identity

F32 = mybir.dt.float32
BF16 = mybir.dt.bfloat16
U32 = mybir.dt.uint32
U8 = mybir.dt.uint8
FP8X4 = mybir.dt.float8_e4m3fn_x4
ACT = mybir.ActivationFunctionType
ALU = mybir.AluOpType

P = 128
PACK = 4
ROWS = 3072
FREQS = 512
PARTS = 2
FEATURES = PARTS * FREQS
ROW_TILES = ROWS // P
PAIR = 2
PAIRS = ROW_TILES // PAIR
EPS = 1e-8
VECTOR_SQUARES = 128
SCALAR_SQUARES = PAIR * FEATURES - VECTOR_SQUARES
TRANSPOSE_LEAD = 2
COPY_LEAD = 1
ADD_LAG = 1
TENSOR_ADD_LAG = 2
ROOT_LAG = 3
QUANTISE_K_LAG = 3
QUANTISE_MAG_LAG = 4
PRODUCT_LAG = 5
FINISH_LAG = 6

FLOPS = 2 * ROWS * P * (FEATURES + FREQS)

TWO_PI = 2.0 * math.pi
TWO_PI_HIGH = 6.28125
TWO_PI_LOW = TWO_PI - TWO_PI_HIGH
ROUND_MAGIC = 1.5 * 2.0**23
SINE = [(-1.0) ** k / math.factorial(2 * k + 1) for k in range(11)]


def in_own_layout(i):
    return i == 0 or i % 4 == 1


def row_tile_groups(i):
    return [slice(0, PAIR)] if i < PAIRS - 1 else [slice(j, j + 1) for j in range(PAIR)]


def exists(i):
    return 0 <= i < PAIRS


def due(s, lag):
    if s - lag == 1:
        return [0, 1]
    return [s - lag] if exists(s - lag) and s > lag else []


def quantise(nc, values, codes, scales):
    nc.vector.quantize_mx(out=codes.bitcast(FP8X4), scales=scales, in_=values)


def sine(nc, pool, theta):
    width = 2 * PACK
    angle = pool.tile([P, width], F32, name="angle")
    for half, offset in ((0, 0.0), (1, 0.5 * math.pi)):
        nc.vector.tensor_scalar(
            out=angle[:, PACK * half : PACK * (half + 1)],
            in0=theta[:],
            scalar1=1.0,
            scalar2=offset,
            op0=ALU.mult,
            op1=ALU.add,
        )
    shifted = pool.tile([P, width], F32, name="shifted")
    nc.vector.tensor_scalar(
        out=shifted[:], in0=angle[:], scalar1=1.0 / TWO_PI, scalar2=ROUND_MAGIC, op0=ALU.mult, op1=ALU.add
    )
    turns = pool.tile([P, width], F32, name="turns")
    nc.vector.tensor_scalar(
        out=turns[:], in0=shifted[:], scalar1=-ROUND_MAGIC, scalar2=1.0, op0=ALU.add, op1=ALU.mult
    )
    x = angle
    for part in (TWO_PI_HIGH, TWO_PI_LOW):
        reduced = pool.tile([P, width], F32, name="reduced")
        nc.vector.scalar_tensor_tensor(
            out=reduced[:], in0=turns[:], scalar=-part, in1=x[:], op0=ALU.mult, op1=ALU.add
        )
        x = reduced
    x_squared = pool.tile([P, width], F32, name="x_squared")
    nc.vector.tensor_tensor(out=x_squared[:], in0=x[:], in1=x[:], op=ALU.mult)
    partial = x_squared
    factor = SINE[-1]
    for k in reversed(range(len(SINE) - 1)):
        series = pool.tile([P, width], F32, name="series")
        nc.gpsimd.tensor_scalar(
            out=series[:], in0=partial[:], scalar1=factor, scalar2=SINE[k], op0=ALU.mult, op1=ALU.add
        )
        product = pool.tile([P, width], F32, name="product")
        nc.gpsimd.tensor_tensor(
            out=product[:], in0=series[:], in1=x_squared[:] if k > 0 else x[:], op=ALU.mult
        )
        partial = product
        factor = 1.0
    return partial


def tile_module2network_kernel(tc, K, reference_angles, probes, u_weights, k_bias, out):
    nc = tc.nc
    with ExitStack() as ctx:
        const = ctx.enter_context(tc.tile_pool(name="const", bufs=1))
        small = ctx.enter_context(tc.tile_pool(name="small", bufs=2))
        k_pool = ctx.enter_context(tc.tile_pool(name="k_in", bufs=PAIRS))
        mx_pool = ctx.enter_context(tc.tile_pool(name="mx", bufs=PAIRS))
        work = ctx.enter_context(tc.tile_pool(name="work", bufs=4))
        own_pool = ctx.enter_context(tc.tile_pool(name="own", bufs=2))
        grouped_pool = ctx.enter_context(
            tc.tile_pool(name="grouped", bufs=COPY_LEAD + QUANTISE_K_LAG + 2)
        )
        k_bank_pool = ctx.enter_context(tc.psum_pool(name="k_bank", bufs=4))
        sum_pool = ctx.enter_context(tc.psum_pool(name="sum", bufs=2))
        acc_pool = ctx.enter_context(tc.psum_pool(name="acc", bufs=2))
        ctx.enter_context(tc.manual_schedule())

        theta = const.tile([P, PACK], BF16)
        nc.sync.dma_start(out=theta[:], in_=reference_angles.rearrange("(p t) -> p t", t=PACK))
        probes_sb = const.tile([P, FEATURES], BF16)
        nc.sync.dma_start(out=probes_sb[:], in_=probes)
        u_sb = const.tile([P, FREQS], BF16)
        k_rows = K.rearrange("(p j) k -> p j k", j=ROW_TILES)
        k_in = []
        for i in range(PAIRS):
            k_pair = k_pool.tile([P, PAIR, FEATURES], BF16, name="k_pair")
            k_in.append(k_pair)
            if i == 0:
                for j in range(PAIR):
                    nc.sync.dma_start(out=k_pair[:, j, :], in_=k_rows[:, j, :])
            else:
                nc.sync.dma_start(out=k_pair[:], in_=k_rows[:, PAIR * i : PAIR * (i + 1), :])
            if i == 1:
                nc.sync.dma_start(out=u_sb[:], in_=u_weights)
        bias_rows = const.tile([P, P], BF16)
        nc.sync.dma_start(out=bias_rows[:], in_=k_bias.partition_broadcast(P))

        zero_col = const.tile([P, 1], F32)
        nc.gpsimd.memset(zero_col[:], 0.0)
        warm_col = const.tile([P, 1], F32)
        nc.scalar.activation(out=warm_col[:], in_=zero_col[:], func=ACT.Sqrt)
        ident = const.tile([P, P], F32)
        make_identity(nc, ident[:])
        eps_col = const.tile([P, 1], F32)
        nc.gpsimd.memset(eps_col[:], EPS)

        k_banks = {}
        k_grouped = {}
        k_codes = {}
        k_scales = {}
        k_squared = {}
        sum_banks = {}
        mag_squared = {}
        mag_grouped = {}
        mag_codes = {}
        mag_scales = {}
        accs = {}
        out_rows = out.rearrange("(p j) b -> p j b", j=ROW_TILES)

        def transpose_k(i):
            if not exists(i):
                return
            k_words = k_in[i][:].bitcast(F32)
            k_banks[i] = {}
            for j in reversed(range(PAIR)):
                k_bank = k_bank_pool.tile([P, PACK, P], F32, name="k_bank")
                for g in range(PARTS):
                    for h in range(2):
                        nc.tensor.transpose(
                            k_bank[:, 2 * g + h, :],
                            k_words[:, j, 2 * P * g + h : 2 * P * (g + 1) : 2],
                            ident[:],
                        )
                k_banks[i][j] = k_bank

        def copy_k(i):
            if not exists(i):
                return
            k_grouped[i] = grouped_pool.tile(
                [P, PAIR, PARTS, P * PACK], BF16, align_bytes=64, name="k_grouped"
            )
            k_grouped_words = k_grouped[i][:].bitcast(F32).rearrange("p j g (n h) -> p j g n h", h=2)
            for j in reversed(range(PAIR)):
                nc.vector.tensor_copy(
                    out=k_grouped_words[:, j],
                    in_=k_banks[i][j][:].rearrange("p (g h) n -> p g n h", g=PARTS),
                )
            if in_own_layout(i):
                return
            k_squared[i] = work.tile([P, PAIR, PARTS, P * PACK], F32, name="k_squared")
            first_row = P - VECTOR_SQUARES // PACK
            last = slice(PACK * first_row, PACK * P)
            nc.vector.tensor_tensor(
                out=k_squared[i][:, PAIR - 1, 1, last].rearrange("p (n h e) -> p n h e", h=2, e=2),
                in0=k_banks[i][PAIR - 1][:]
                .bitcast(BF16)[:, 2:PACK, 2 * first_row :]
                .rearrange("p h (n e) -> p n h e", e=2),
                in1=k_grouped[i][:, PAIR - 1, 1, last].rearrange("p (n h e) -> p n h e", h=2, e=2),
                op=ALU.mult,
            )

        def squares(i):
            if not exists(i):
                return
            if in_own_layout(i):
                k_squared[i] = own_pool.tile([P, PAIR, PARTS, PACK, P], F32, name="k_own_squared")
                nc.scalar.activation(
                    out=k_squared[i][:].rearrange("r j g t q -> r (j g) t q"),
                    in_=k_in[i][:].rearrange("r j (g q t) -> r (j g) t q", g=PARTS, t=PACK),
                    func=ACT.Square,
                )
                return
            out_flat = k_squared[i][:].rearrange("p j g w -> p (j g w)")
            in_flat = k_grouped[i][:].rearrange("p j g w -> p (j g w)")
            for js in row_tile_groups(i):
                cols = slice(js.start * FEATURES, min(js.stop * FEATURES, SCALAR_SQUARES))
                nc.scalar.activation(out=out_flat[:, cols], in_=in_flat[:, cols], func=ACT.Square)

        def add_on_tensor(i):
            if not exists(i) or not in_own_layout(i):
                return
            sum_banks[i] = {}
            for j in range(PAIR):
                sum_bank = sum_pool.tile([P, PACK, P], F32, tag="sum", name="sum_bank")
                for t in range(PACK):
                    for g in range(PARTS):
                        nc.tensor.matmul(
                            sum_bank[:, t, :],
                            lhsT=k_squared[i][:, j, g, t, :],
                            rhs=ident[:],
                            is_transpose=True,
                            start=(g == 0),
                            stop=(g == PARTS - 1),
                        )
                sum_banks[i][j] = sum_bank

        def add(i):
            if not exists(i) or in_own_layout(i):
                return
            mag_squared[i] = work.tile([P, PAIR, P * PACK], F32, name="mag_squared")
            quantised = i + ADD_LAG - 1 - QUANTISE_K_LAG
            if exists(quantised):
                gate = small.tile([P, 1], U32, name="gate")
                nc.gpsimd.tensor_copy(out=gate[:], in_=k_codes[quantised][:, 0, 0, 0:1])
            for j in range(PAIR):
                engine = nc.gpsimd if j == 0 and i < PAIRS - 1 else nc.vector
                engine.tensor_tensor(
                    out=mag_squared[i][:, j, :],
                    in0=k_squared[i][:, j, 0, :],
                    in1=k_squared[i][:, j, 1, :],
                    op=ALU.add,
                )

        def roots(i):
            if not exists(i):
                return
            mag_grouped[i] = work.tile([P, PAIR, P * PACK], BF16, align_bytes=64, name="mag_grouped")
            if in_own_layout(i):
                for j in range(PAIR):
                    nc.scalar.activation(
                        out=mag_grouped[i][:, j, :].rearrange("p (n t) -> p n t", t=PACK),
                        in_=sum_banks[i][j][:].rearrange("p t n -> p n t"),
                        func=ACT.Sqrt,
                        bias=eps_col[:, 0:1],
                    )
                return
            for js in row_tile_groups(i):
                nc.scalar.activation(
                    out=mag_grouped[i][:, js, :],
                    in_=mag_squared[i][:, js, :],
                    func=ACT.Sqrt,
                    bias=eps_col[:, 0:1],
                )

        def quantise_mag(i):
            if not exists(i):
                return
            mag_codes[i] = mx_pool.tile([P, PAIR, P], U32, align_bytes=64, name="mag_codes")
            mag_scales[i] = mx_pool.tile([P, PAIR, P], U8, align_bytes=64, name="mag_scales")
            for js in row_tile_groups(i):
                quantise(
                    nc,
                    mag_grouped[i][:, js, :].rearrange("p j w -> p (j w)"),
                    mag_codes[i][:, js, :].rearrange("p j n -> p (j n)"),
                    mag_scales[i][:, js, :].rearrange("p j n -> p (j n)"),
                )

        def quantise_k(i):
            if not exists(i):
                return
            k_codes[i] = mx_pool.tile([P, PAIR, PARTS, P], U32, align_bytes=64, name="k_codes")
            k_scales[i] = mx_pool.tile([P, PAIR, PARTS, P], U8, align_bytes=64, name="k_scales")
            quantise(
                nc,
                k_grouped[i][:].rearrange("p j g w -> p (j g w)"),
                k_codes[i][:].rearrange("p j g n -> p (j g n)"),
                k_scales[i][:].rearrange("p j g n -> p (j g n)"),
            )

        def products(i):
            if not exists(i):
                return
            accs[i] = []
            for js in row_tile_groups(i):
                acc = acc_pool.tile([P, js.stop - js.start, P], F32, tag="acc", name="acc")
                accs[i].append(acc)
                for j in range(js.start, js.stop):
                    for g in range(PARTS):
                        nc.tensor.matmul_mx(
                            out=acc[:, j - js.start, :],
                            lhsT=k_codes[i][:, j, g, :].bitcast(FP8X4),
                            lhsT_scale=k_scales[i][:, j, g, :],
                            rhs=rot_codes[:, g, :].bitcast(FP8X4),
                            rhs_scale=rot_scales[:, g, :],
                            start=(g == 0),
                            stop=False,
                        )
                    nc.tensor.matmul_mx(
                        out=acc[:, j - js.start, :],
                        lhsT=mag_codes[i][:, j, :].bitcast(FP8X4),
                        lhsT_scale=mag_scales[i][:, j, :],
                        rhs=u_codes[:].bitcast(FP8X4),
                        rhs_scale=u_scales[:],
                        start=False,
                        stop=True,
                    )

        def finish(i):
            if not exists(i):
                return
            for js, acc in zip(row_tile_groups(i), accs[i]):
                n = js.stop - js.start
                logits = work.tile([P, n, P], F32, name="logits")
                bias_b = bias_rows[:].unsqueeze(1).to_broadcast([P, n, P])
                nc.vector.tensor_tensor(out=logits[:], in0=acc[:], in1=bias_b, op=ALU.add)
                nc.sync.dma_start(
                    out=out_rows[:, PAIR * i + js.start : PAIR * i + js.stop, :], in_=logits[:]
                )

        def step_on_psum(s):
            copy_k(s + COPY_LEAD)
            transpose_k(s + TRANSPOSE_LEAD)
            for i in due(s, FINISH_LAG):
                finish(i)
            squares(s)

        def step_on_sbuf(s):
            add_on_tensor(s - TENSOR_ADD_LAG)
            add(s - ADD_LAG)
            roots(s - ROOT_LAG)
            quantise_mag(s - QUANTISE_MAG_LAG)
            quantise_k(s - QUANTISE_K_LAG)
            for i in due(s, PRODUCT_LAG):
                products(i)

        sin_cos = sine(nc, small, theta)

        probes_squared = const.tile([P, FEATURES], BF16)
        sum_squares = const.tile([P, 1], F32)
        nc.scalar.activation(
            out=probes_squared[:], in_=probes_sb[:], func=ACT.Square, accum_out=sum_squares[:]
        )
        norm = const.tile([P, 1], F32)
        nc.scalar.activation(out=norm[:], in_=sum_squares[:], func=ACT.Sqrt)
        norm_eps = const.tile([P, 1], F32)
        nc.vector.tensor_scalar_add(out=norm_eps[:], in0=norm[:], scalar1=EPS)
        inv_norm = const.tile([P, 1], F32)
        nc.vector.reciprocal(out=inv_norm[:], in_=norm_eps[:])
        p_unit = const.tile([P, PARTS, PACK, P], F32)
        nc.vector.tensor_scalar_mul(
            out=p_unit[:],
            in0=probes_sb[:].rearrange("b (g q t) -> b g t q", g=PARTS, t=PACK),
            scalar1=inv_norm[:, 0:1],
        )

        transpose_k(0)
        transpose_k(1)
        p_banks = []
        for g in range(PARTS):
            p_bank = acc_pool.tile([P, PACK, P], F32, tag="acc", name="p_bank")
            for t in range(PACK):
                nc.tensor.transpose(p_bank[:, t, :], p_unit[:, g, t, :], ident[:])
            p_banks.append(p_bank)

        copy_k(0)
        step_on_psum(0)
        step_on_sbuf(0)
        step_on_psum(1)

        u_words = u_sb[:].bitcast(F32)
        u_bank = sum_pool.tile([P, PACK, P], F32, tag="sum", name="u_bank")
        for h in range(2):
            nc.tensor.transpose(u_bank[:, h, :], u_words[:, h : 2 * P : 2], ident[:])
        u_grouped = const.tile([P, P, PACK], BF16, align_bytes=64)
        nc.vector.tensor_copy(
            out=u_grouped[:].bitcast(F32), in_=u_bank[:, 0:2, :].rearrange("p h b -> p b h")
        )

        step_on_sbuf(1)
        step_on_psum(2)

        u_codes = const.tile([P, P], U32, align_bytes=64)
        u_scales = const.tile([P, P], U8, align_bytes=64)
        quantise(nc, u_grouped[:].rearrange("p b t -> p (b t)"), u_codes[:], u_scales[:])

        step_on_sbuf(2)
        step_on_psum(3)

        sin_b = sin_cos[:, 0:PACK].unsqueeze(1).to_broadcast([P, P, PACK])
        cos_b = sin_cos[:, PACK : 2 * PACK].unsqueeze(1).to_broadcast([P, P, PACK])
        p_words = [p_bank[:].rearrange("p t b -> p b t") for p_bank in p_banks]
        rot_grouped = const.tile([P, PARTS, P, PACK], BF16, align_bytes=64)
        re_cos = const.tile([P, P, PACK], F32)
        nc.vector.tensor_tensor(out=re_cos[:], in0=p_words[0], in1=cos_b, op=ALU.mult)
        im_sin = const.tile([P, P, PACK], F32)
        nc.vector.tensor_tensor(out=im_sin[:], in0=p_words[1], in1=sin_b, op=ALU.mult)
        nc.gpsimd.tensor_tensor(
            out=rot_grouped[:, 0], in0=re_cos[:], in1=im_sin[:], op=ALU.subtract
        )

        step_on_sbuf(3)
        step_on_psum(4)

        im_cos = const.tile([P, P, PACK], F32)
        nc.vector.tensor_tensor(out=im_cos[:], in0=p_words[1], in1=cos_b, op=ALU.mult)
        re_sin = const.tile([P, P, PACK], F32)
        nc.vector.tensor_tensor(out=re_sin[:], in0=p_words[0], in1=sin_b, op=ALU.mult)
        nc.gpsimd.tensor_tensor(out=rot_grouped[:, 1], in0=im_cos[:], in1=re_sin[:], op=ALU.add)

        step_on_sbuf(4)
        step_on_psum(5)

        rot_codes = const.tile([P, PARTS, P], U32, align_bytes=64)
        rot_scales = const.tile([P, PARTS, P], U8, align_bytes=64)
        quantise(
            nc,
            rot_grouped[:].rearrange("p g b t -> p (g b t)"),
            rot_codes[:].rearrange("p g b -> p (g b)"),
            rot_scales[:].rearrange("p g b -> p (g b)"),
        )

        step_on_sbuf(5)

        for s in range(PRODUCT_LAG + 1, PAIRS + FINISH_LAG):
            step_on_psum(s)
            step_on_sbuf(s)
